import numpy as np
import ml_dtypes


def mxq(x, axis, fmt="e4m3"):
    dtype, down = {"e4m3": (ml_dtypes.float8_e4m3fn, 7), "e5m2": (ml_dtypes.float8_e5m2, 14)}[fmt]
    v = np.moveaxis(np.asarray(x, np.float32).astype(ml_dtypes.bfloat16).astype(np.float64), axis, -1)
    blocks = v.reshape(v.shape[:-1] + (-1, 32))
    amax = np.abs(blocks).max(-1, keepdims=True)
    byte = np.maximum(np.where(amax > 0, np.frexp(amax)[1] - 1 + 127, 0) - down, 1)
    scale = np.exp2(byte - 127.0)
    codes = (blocks / scale).astype(np.float32).astype(dtype).astype(np.float64)
    return np.moveaxis((codes * scale).reshape(v.shape), -1, axis)


WIDE = False


def mx_kscale(k):
    if not WIDE:
        return np.ones(k)
    levels = np.array([10, -10, 5, -5, 0])
    a = np.random.permutation(np.resize(levels, k // 512 * 4)).reshape(k // 512, 4)
    idx = np.arange(k)
    return np.exp2(a[idx // 512, idx % 128 // 32])


BF16 = ml_dtypes.bfloat16


def bf(x):
    return np.asarray(x, np.float32).astype(BF16)


def f64(x):
    return np.asarray(x).astype(np.float64)


E2M1 = np.array([0.0, 0.5, 1.0, 1.5, 2.0, 3.0, 4.0, 6.0, -0.0, -0.5, -1.0, -1.5, -2.0, -3.0, -4.0, -6.0])


def pack_weight(w, fmt):
    k, n = w.shape
    w = f64(bf(w)).reshape(k // 32, 32, n)
    amax = np.abs(w).max(1)
    if fmt == "e4m3":
        byte = np.frexp(amax)[1] - 1 + 127 - 7
    else:
        mant, ex = np.frexp(amax / 6.0)
        byte = np.where(mant > 0.5, ex, ex - 1) + 127
    byte = np.clip(np.where(amax > 0, byte, 1), 1, 254)
    scaled = (w * np.exp2(127.0 - byte)[:, None, :]).reshape(k, n).astype(np.float32)
    by_word = np.ascontiguousarray(scaled.reshape(k // 512, 128, 4, n).transpose(0, 1, 3, 2))
    if fmt == "e4m3":
        words = by_word.astype(ml_dtypes.float8_e4m3fn).view(np.uint8)
    else:
        c = by_word.astype(ml_dtypes.float4_e2m1fn).view(np.uint8) & 0xF
        words = c[..., 0::2] | (c[..., 1::2] << 4)
    return np.ascontiguousarray(words), np.ascontiguousarray(byte.astype(np.uint8).reshape(k // 512, 16, n))


def unpack_weight(words, scales, fmt):
    g, p, n, _ = words.shape
    if fmt == "e4m3":
        vals = np.ascontiguousarray(words).view(ml_dtypes.float8_e4m3fn).astype(np.float64)
    else:
        nib = np.empty((g, p, n, 4), np.uint8)
        nib[..., 0::2] = words & 0xF
        nib[..., 1::2] = words >> 4
        vals = E2M1[nib]
    vals = vals * np.repeat(np.exp2(scales.astype(np.float64) - 127.0), 8, axis=1)[..., None]
    return vals.transpose(0, 1, 3, 2).reshape(g * 512, n)


N, S, I, L, M = 128, 8, 512, 512, 256
D = I + L
FMT = "e4m3"


def sigmoid(v):
    return 1.0 / (1.0 + np.exp(-v))


def pack_stack(w):
    cat = np.ascontiguousarray(w.swapaxes(1, 2)).reshape(-1, L)
    return pack_weight(cat, FMT)


def setup_inputs():
    s = mx_kscale(D)
    r = np.random.standard_normal
    modulation = bf((r((N, S, I)) * s[:I]).reshape(N, S * I))
    h0 = bf((r((N, S, L)) * s[I:]).reshape(N, S * L))
    c0 = bf(r((N, S * L)))
    Wi_words, Wi_scales = pack_stack(r((S, L, D)) / np.sqrt(D) / s)
    b_i = bf(-1.0 + 0.3 * r((S, L)))
    Wf_words, Wf_scales = pack_stack(r((S, L, D)) / np.sqrt(D) / s)
    b_f = bf(1.0 + 0.3 * r((S, L)))
    Wg_words, Wg_scales = pack_stack(r((S, L, D)) / np.sqrt(D) / s)
    b_g = bf(0.3 * r((S, L)))
    return {"modulation": modulation,
            "h0": h0,
            "c0": c0,
            "Wi_words": Wi_words, "Wi_scales": Wi_scales, "b_i": b_i,
            "Wf_words": Wf_words, "Wf_scales": Wf_scales, "b_f": b_f,
            "Wg_words": Wg_words, "Wg_scales": Wg_scales, "b_g": b_g}


def proj(xq, words, scales, b):
    return (xq.transpose(1, 0, 2) @ unpack_weight(words, scales, FMT).reshape(S, D, L)).transpose(1, 0, 2) + f64(b)


def reference(modulation, h0, c0, Wi_words, Wi_scales, b_i, Wf_words, Wf_scales, b_f, Wg_words, Wg_scales, b_g):
    x = f64(modulation).reshape(N, S, I)
    h = f64(h0).reshape(N, S, L)
    c = f64(c0).reshape(N, S, L)
    xq = mxq(np.concatenate([x, h], axis=-1), 2, "e4m3")
    i = sigmoid(proj(xq, Wi_words, Wi_scales, b_i))
    f = sigmoid(proj(xq, Wf_words, Wf_scales, b_f))
    g = np.tanh(proj(xq, Wg_words, Wg_scales, b_g))
    return (f * c + i * g).reshape(N, S * L)

@@ -1,0 +1,150 @@
+from contextlib import ExitStack
+
+import concourse.mybir as mybir
+from concourse.masks import make_identity
+
+BF16 = mybir.dt.bfloat16
+F32 = mybir.dt.float32
+I32 = mybir.dt.int32
+U32 = mybir.dt.uint32
+U8 = mybir.dt.uint8
+FP8X4 = mybir.dt.float8_e4m3fn_x4
+SIGMOID = mybir.ActivationFunctionType.Sigmoid
+TANH = mybir.ActivationFunctionType.Tanh
+
+P = 128
+PACK = 4
+STREAMS = 8
+FEAT = 512
+HALVES = 2
+GROUPS = STREAMS * HALVES
+CHUNKS = FEAT // P
+QUADS = 4
+PAIR = 2
+
+FLOPS = 2 * P * STREAMS * (HALVES * FEAT) * FEAT * 3
+
+
+def tile_flatlstm_pa_e_kernel(
+    tc, modulation, h0, c0, Wi_words, Wi_scales, b_i, Wf_words, Wf_scales, b_f, Wg_words, Wg_scales, b_g, out
+):
+    nc = tc.nc
+    gates = (
+        ("i", Wi_words, Wi_scales, b_i, SIGMOID),
+        ("g", Wg_words, Wg_scales, b_g, TANH),
+        ("f", Wf_words, Wf_scales, b_f, SIGMOID),
+    )
+
+    with ExitStack() as pools:
+        keep = pools.enter_context(tc.tile_pool(name="keep", bufs=1))
+        work = pools.enter_context(tc.tile_pool(name="work", bufs=3))
+        done = pools.enter_context(tc.tile_pool(name="done", bufs=STREAMS))
+        psum = pools.enter_context(tc.psum_pool(name="psum", bufs=8))
+
+        x_rows = keep.tile([P, STREAMS * FEAT], BF16)
+        h_rows = keep.tile([P, STREAMS * FEAT], BF16)
+        c_rows = keep.tile([P, STREAMS * FEAT], BF16)
+        nc.sync.dma_start(out=x_rows[:], in_=modulation)
+        nc.sync.dma_start(out=h_rows[:], in_=h0)
+
+        w_planes = keep.tile([P, GROUPS, FEAT], U8, align_bytes=64)
+        nc.vector.memset(w_planes[:].bitcast(I32), 0)
+        for j, (gate, words, scales, bias, func) in enumerate(gates):
+            for quad in range(QUADS):
+                first = 32 * quad + 4 * j
+                nc.sync.dma_start(
+                    out=w_planes[first : first + 4].bitcast(I32),
+                    in_=scales[:, 4 * quad : 4 * quad + 4, :].rearrange("g r n -> r g n").bitcast(I32),
+                )
+
+        w_words = {}
+        for s in range(STREAMS):
+            for gate, words, scales, bias, func in gates:
+                w_tile = keep.tile([P, HALVES, FEAT], U32, name="w_%s%d" % (gate, s), align_bytes=64)
+                nc.sync.dma_start(
+                    out=w_tile[:].bitcast(I32),
+                    in_=words[HALVES * s : HALVES * (s + 1)].rearrange("g p n t -> p g (n t)").bitcast(I32),
+                )
+                w_words[(gate, s)] = w_tile
+            if s == 0:
+                nc.sync.dma_start(out=c_rows[:], in_=c0)
+
+        identity = keep.tile([P, P], F32)
+        make_identity(nc, identity[:])
+
+        bias_rows = keep.tile([P, P], BF16)
+        nc.vector.memset(bias_rows[:], 0.0)
+        for j, (gate, words, scales, bias, func) in enumerate(gates):
+            nc.scalar.dma_start(
+                out=bias_rows[32 * j : 32 * (j + 1), :], in_=bias.rearrange("s (c l) -> (s c) l", l=P)
+            )
+        bias_rows_f32 = keep.tile([P, P], F32)
+        nc.vector.tensor_copy(out=bias_rows_f32[:], in_=bias_rows[:])
+        bias_bank = psum.tile([P, CHUNKS, P], F32, tag="bank")
+        nc.tensor.transpose(bias_bank[:, 0, :], bias_rows_f32[:], identity[:])
+        bias_cols = keep.tile([P, P], F32)
+        nc.vector.tensor_copy(out=bias_cols[:], in_=bias_bank[:, 0, :])
+
+        x_codes = keep.tile([P, STREAMS, HALVES * P], U32, align_bytes=64)
+        x_planes = keep.tile([P, STREAMS, HALVES * P], U8, align_bytes=64)
+        words_in_group = FEAT // PAIR
+        for s in range(STREAMS):
+            flipped = psum.tile([P, HALVES * PAIR, P], F32, tag="bank")
+            for half, rows in enumerate((x_rows, h_rows)):
+                group_words = rows[:].bitcast(F32)[:, words_in_group * s : words_in_group * (s + 1)]
+                for u in range(PAIR):
+                    nc.tensor.transpose(flipped[:, PAIR * half + u, :], group_words[:, u::PAIR], identity[:])
+            grouped = work.tile([P, HALVES * P * PACK], BF16, align_bytes=64)
+            nc.scalar.copy(
+                out=grouped[:].bitcast(F32).rearrange("p (h n u) -> p h n u", h=HALVES, u=PAIR),
+                in_=flipped[:].rearrange("p (h u) n -> p h n u", u=PAIR),
+            )
+            nc.vector.quantize_mx(
+                out=x_codes[:, s, :].bitcast(FP8X4), scales=x_planes[:, s, :], in_=grouped[:]
+            )
+
+        for s in range(STREAMS):
+            acted = {}
+            for j, (gate, words, scales, bias, func) in enumerate(gates):
+                acc = psum.tile([P, CHUNKS, P], F32, tag="bank")
+                for c in range(CHUNKS):
+                    for half in range(HALVES):
+                        nc.tensor.matmul_mx(
+                            out=acc[:, c, :],
+                            lhsT=w_words[(gate, s)][:, half, P * c : P * (c + 1)].bitcast(FP8X4),
+                            lhsT_scale=w_planes[4 * j : P, HALVES * s + half, P * c : P * (c + 1)],
+                            rhs=x_codes[:, s, P * half : P * (half + 1)].bitcast(FP8X4),
+                            rhs_scale=x_planes[:, s, P * half : P * (half + 1)],
+                            start=(half == 0),
+                            stop=(half == HALVES - 1),
+                        )
+                gate_t = work.tile([P, CHUNKS, P], F32, name="gate_%s" % gate)
+                for c in range(CHUNKS):
+                    column = 32 * j + CHUNKS * s + c
+                    nc.scalar.activation(
+                        out=gate_t[:, c, :],
+                        in_=acc[:, c, :],
+                        func=func,
+                        bias=bias_cols[:, column : column + 1],
+                        scale=1.0,
+                    )
+                acted[gate] = gate_t
+
+            ig_t = work.tile([P, CHUNKS, P], F32)
+            nc.vector.tensor_mul(out=ig_t[:], in0=acted["i"][:], in1=acted["g"][:])
+
+            ig_rows = psum.tile([P, CHUNKS, P], F32, tag="bank")
+            f_rows = psum.tile([P, CHUNKS, P], F32, tag="bank")
+            for c in range(CHUNKS):
+                nc.tensor.transpose(ig_rows[:, c, :], ig_t[:, c, :], identity[:])
+            for c in range(CHUNKS):
+                nc.tensor.transpose(f_rows[:, c, :], acted["f"][:, c, :], identity[:])
+
+            stream_cols = slice(FEAT * s, FEAT * (s + 1))
+            fc = work.tile([P, FEAT], F32)
+            nc.vector.tensor_mul(
+                out=fc[:], in0=f_rows[:].rearrange("n c l -> n (c l)"), in1=c_rows[:, stream_cols]
+            )
+            c_new = done.tile([P, FEAT], F32)
+            nc.vector.tensor_add(out=c_new[:], in0=fc[:], in1=ig_rows[:].rearrange("n c l -> n (c l)"))
+            nc.sync.dma_start(out=out[:, stream_cols], in_=c_new[:])

@@ -40,6 +40,7 @@ def tile_flatlstm_pa_e_kernel(
         work = pools.enter_context(tc.tile_pool(name="work", bufs=3))
         done = pools.enter_context(tc.tile_pool(name="done", bufs=STREAMS))
         psum = pools.enter_context(tc.psum_pool(name="psum", bufs=8))
+        pools.enter_context(tc.manual_schedule())
 
         x_rows = keep.tile([P, STREAMS * FEAT], BF16)
         h_rows = keep.tile([P, STREAMS * FEAT], BF16)
@@ -103,43 +104,40 @@ def tile_flatlstm_pa_e_kernel(
                 out=x_codes[:, s, :].bitcast(FP8X4), scales=x_planes[:, s, :], in_=grouped[:]
             )
 
-        for s in range(STREAMS):
-            acted = {}
-            for j, (gate, words, scales, bias, func) in enumerate(gates):
-                acc = psum.tile([P, CHUNKS, P], F32, tag="bank")
-                for c in range(CHUNKS):
-                    for half in range(HALVES):
-                        nc.tensor.matmul_mx(
-                            out=acc[:, c, :],
-                            lhsT=w_words[(gate, s)][:, half, P * c : P * (c + 1)].bitcast(FP8X4),
-                            lhsT_scale=w_planes[4 * j : P, HALVES * s + half, P * c : P * (c + 1)],
-                            rhs=x_codes[:, s, P * half : P * (half + 1)].bitcast(FP8X4),
-                            rhs_scale=x_planes[:, s, P * half : P * (half + 1)],
-                            start=(half == 0),
-                            stop=(half == HALVES - 1),
-                        )
-                gate_t = work.tile([P, CHUNKS, P], F32, name="gate_%s" % gate)
-                for c in range(CHUNKS):
-                    column = 32 * j + CHUNKS * s + c
-                    nc.scalar.activation(
-                        out=gate_t[:, c, :],
-                        in_=acc[:, c, :],
-                        func=func,
-                        bias=bias_cols[:, column : column + 1],
-                        scale=1.0,
+        def gate_of_stream(s, j):
+            gate, words, scales, bias, func = gates[j]
+            acc = psum.tile([P, CHUNKS, P], F32, tag="bank")
+            for c in range(CHUNKS):
+                for half in range(HALVES):
+                    nc.tensor.matmul_mx(
+                        out=acc[:, c, :],
+                        lhsT=w_words[(gate, s)][:, half, P * c : P * (c + 1)].bitcast(FP8X4),
+                        lhsT_scale=w_planes[4 * j : P, HALVES * s + half, P * c : P * (c + 1)],
+                        rhs=x_codes[:, s, P * half : P * (half + 1)].bitcast(FP8X4),
+                        rhs_scale=x_planes[:, s, P * half : P * (half + 1)],
+                        start=(half == 0),
+                        stop=(half == HALVES - 1),
                     )
-                acted[gate] = gate_t
-
-            ig_t = work.tile([P, CHUNKS, P], F32)
-            nc.vector.tensor_mul(out=ig_t[:], in0=acted["i"][:], in1=acted["g"][:])
-
-            ig_rows = psum.tile([P, CHUNKS, P], F32, tag="bank")
-            f_rows = psum.tile([P, CHUNKS, P], F32, tag="bank")
+            gate_t = work.tile([P, CHUNKS, P], F32, name="gate_%s" % gate)
             for c in range(CHUNKS):
-                nc.tensor.transpose(ig_rows[:, c, :], ig_t[:, c, :], identity[:])
-            for c in range(CHUNKS):
-                nc.tensor.transpose(f_rows[:, c, :], acted["f"][:, c, :], identity[:])
+                column = 32 * j + CHUNKS * s + c
+                nc.scalar.activation(
+                    out=gate_t[:, c, :],
+                    in_=acc[:, c, :],
+                    func=func,
+                    bias=bias_cols[:, column : column + 1],
+                    scale=1.0,
+                )
+            return gate_t
 
+        def to_rows(feature_major):
+            rows = psum.tile([P, CHUNKS, P], F32, tag="bank")
+            for c in range(CHUNKS):
+                nc.tensor.transpose(rows[:, c, :], feature_major[:, c, :], identity[:])
+            return rows
+
+        def finish_stream(s, f_t, ig_rows):
+            f_rows = to_rows(f_t)
             stream_cols = slice(FEAT * s, FEAT * (s + 1))
             fc = work.tile([P, FEAT], F32)
             nc.vector.tensor_mul(
@@ -148,3 +146,15 @@ def tile_flatlstm_pa_e_kernel(
             c_new = done.tile([P, FEAT], F32)
             nc.vector.tensor_add(out=c_new[:], in0=fc[:], in1=ig_rows[:].rearrange("n c l -> n (c l)"))
             nc.sync.dma_start(out=out[:, stream_cols], in_=c_new[:])
+
+        unfinished = None
+        for s in range(STREAMS):
+            i_t = gate_of_stream(s, 0)
+            if unfinished is not None:
+                finish_stream(s - 1, unfinished[0], unfinished[1])
+            g_t = gate_of_stream(s, 1)
+            ig_t = work.tile([P, CHUNKS, P], F32)
+            nc.vector.tensor_mul(out=ig_t[:], in0=i_t[:], in1=g_t[:])
+            f_t = gate_of_stream(s, 2)
+            unfinished = (f_t, to_rows(ig_t))
+        finish_stream(STREAMS - 1, unfinished[0], unfinished[1])

@@ -40,7 +40,9 @@ def tile_flatlstm_pa_e_kernel(
         work = pools.enter_context(tc.tile_pool(name="work", bufs=3))
         done = pools.enter_context(tc.tile_pool(name="done", bufs=STREAMS))
         psum = pools.enter_context(tc.psum_pool(name="psum", bufs=8))
-        pools.enter_context(tc.manual_schedule())
+
+        identity = keep.tile([P, P], F32)
+        make_identity(nc, identity[:])
 
         x_rows = keep.tile([P, STREAMS * FEAT], BF16)
         h_rows = keep.tile([P, STREAMS * FEAT], BF16)
@@ -53,9 +55,9 @@ def tile_flatlstm_pa_e_kernel(
         for j, (gate, words, scales, bias, func) in enumerate(gates):
             for quad in range(QUADS):
                 first = 32 * quad + 4 * j
-                nc.sync.dma_start(
-                    out=w_planes[first : first + 4].bitcast(I32),
-                    in_=scales[:, 4 * quad : 4 * quad + 4, :].rearrange("g r n -> r g n").bitcast(I32),
+                nc.gpsimd.dma_start(
+                    out=w_planes[first : first + 4].bitcast(F32),
+                    in_=scales[:, 4 * quad : 4 * quad + 4, :].rearrange("g r n -> r g n").bitcast(F32),
                 )
 
         w_words = {}
@@ -69,9 +71,6 @@ def tile_flatlstm_pa_e_kernel(
                 w_words[(gate, s)] = w_tile
             if s == 0:
                 nc.sync.dma_start(out=c_rows[:], in_=c0)
-
-        identity = keep.tile([P, P], F32)
-        make_identity(nc, identity[:])
 
         bias_rows = keep.tile([P, P], BF16)
         nc.vector.memset(bias_rows[:], 0.0)
@@ -104,40 +103,43 @@ def tile_flatlstm_pa_e_kernel(
                 out=x_codes[:, s, :].bitcast(FP8X4), scales=x_planes[:, s, :], in_=grouped[:]
             )
 
-        def gate_of_stream(s, j):
-            gate, words, scales, bias, func = gates[j]
-            acc = psum.tile([P, CHUNKS, P], F32, tag="bank")
-            for c in range(CHUNKS):
-                for half in range(HALVES):
-                    nc.tensor.matmul_mx(
-                        out=acc[:, c, :],
-                        lhsT=w_words[(gate, s)][:, half, P * c : P * (c + 1)].bitcast(FP8X4),
-                        lhsT_scale=w_planes[4 * j : P, HALVES * s + half, P * c : P * (c + 1)],
-                        rhs=x_codes[:, s, P * half : P * (half + 1)].bitcast(FP8X4),
-                        rhs_scale=x_planes[:, s, P * half : P * (half + 1)],
-                        start=(half == 0),
-                        stop=(half == HALVES - 1),
+        for s in range(STREAMS):
+            acted = {}
+            for j, (gate, words, scales, bias, func) in enumerate(gates):
+                acc = psum.tile([P, CHUNKS, P], F32, tag="bank")
+                for c in range(CHUNKS):
+                    for half in range(HALVES):
+                        nc.tensor.matmul_mx(
+                            out=acc[:, c, :],
+                            lhsT=w_words[(gate, s)][:, half, P * c : P * (c + 1)].bitcast(FP8X4),
+                            lhsT_scale=w_planes[4 * j : P, HALVES * s + half, P * c : P * (c + 1)],
+                            rhs=x_codes[:, s, P * half : P * (half + 1)].bitcast(FP8X4),
+                            rhs_scale=x_planes[:, s, P * half : P * (half + 1)],
+                            start=(half == 0),
+                            stop=(half == HALVES - 1),
+                        )
+                gate_t = work.tile([P, CHUNKS, P], F32, name="gate_%s" % gate)
+                for c in range(CHUNKS):
+                    column = 32 * j + CHUNKS * s + c
+                    nc.scalar.activation(
+                        out=gate_t[:, c, :],
+                        in_=acc[:, c, :],
+                        func=func,
+                        bias=bias_cols[:, column : column + 1],
+                        scale=1.0,
                     )
-            gate_t = work.tile([P, CHUNKS, P], F32, name="gate_%s" % gate)
-            for c in range(CHUNKS):
-                column = 32 * j + CHUNKS * s + c
-                nc.scalar.activation(
-                    out=gate_t[:, c, :],
-                    in_=acc[:, c, :],
-                    func=func,
-                    bias=bias_cols[:, column : column + 1],
-                    scale=1.0,
-                )
-            return gate_t
+                acted[gate] = gate_t
 
-        def to_rows(feature_major):
-            rows = psum.tile([P, CHUNKS, P], F32, tag="bank")
-            for c in range(CHUNKS):
-                nc.tensor.transpose(rows[:, c, :], feature_major[:, c, :], identity[:])
-            return rows
+            ig_t = work.tile([P, CHUNKS, P], F32)
+            nc.vector.tensor_mul(out=ig_t[:], in0=acted["i"][:], in1=acted["g"][:])
 
-        def finish_stream(s, f_t, ig_rows):
-            f_rows = to_rows(f_t)
+            ig_rows = psum.tile([P, CHUNKS, P], F32, tag="bank")
+            f_rows = psum.tile([P, CHUNKS, P], F32, tag="bank")
+            for c in range(CHUNKS):
+                nc.tensor.transpose(ig_rows[:, c, :], ig_t[:, c, :], identity[:])
+            for c in range(CHUNKS):
+                nc.tensor.transpose(f_rows[:, c, :], acted["f"][:, c, :], identity[:])
+
             stream_cols = slice(FEAT * s, FEAT * (s + 1))
             fc = work.tile([P, FEAT], F32)
             nc.vector.tensor_mul(
@@ -146,15 +148,3 @@ def tile_flatlstm_pa_e_kernel(
             c_new = done.tile([P, FEAT], F32)
             nc.vector.tensor_add(out=c_new[:], in0=fc[:], in1=ig_rows[:].rearrange("n c l -> n (c l)"))
             nc.sync.dma_start(out=out[:, stream_cols], in_=c_new[:])
-
-        unfinished = None
-        for s in range(STREAMS):
-            i_t = gate_of_stream(s, 0)
-            if unfinished is not None:
-                finish_stream(s - 1, unfinished[0], unfinished[1])
-            g_t = gate_of_stream(s, 1)
-            ig_t = work.tile([P, CHUNKS, P], F32)
-            nc.vector.tensor_mul(out=ig_t[:], in0=i_t[:], in1=g_t[:])
-            f_t = gate_of_stream(s, 2)
-            unfinished = (f_t, to_rows(ig_t))
-        finish_stream(STREAMS - 1, unfinished[0], unfinished[1])

@@ -40,9 +40,26 @@ def tile_flatlstm_pa_e_kernel(
         work = pools.enter_context(tc.tile_pool(name="work", bufs=3))
         done = pools.enter_context(tc.tile_pool(name="done", bufs=STREAMS))
         psum = pools.enter_context(tc.psum_pool(name="psum", bufs=8))
+        pools.enter_context(tc.manual_schedule())
 
         identity = keep.tile([P, P], F32)
         make_identity(nc, identity[:])
+
+        bias_rows = keep.tile([P, P], BF16)
+        w_planes = keep.tile([P, GROUPS, FEAT], U8, align_bytes=64)
+        nc.vector.memset(bias_rows[:], 0.0)
+        nc.vector.memset(w_planes[:].bitcast(I32), 0)
+
+        for j, (gate, words, scales, bias, func) in enumerate(gates):
+            nc.sync.dma_start(
+                out=bias_rows[32 * j : 32 * (j + 1), :], in_=bias.rearrange("s (c l) -> (s c) l", l=P)
+            )
+        bias_rows_f32 = keep.tile([P, P], F32)
+        nc.vector.tensor_copy(out=bias_rows_f32[:], in_=bias_rows[:])
+        bias_bank = psum.tile([P, CHUNKS, P], F32, tag="bank")
+        nc.tensor.transpose(bias_bank[:, 0, :], bias_rows_f32[:], identity[:])
+        bias_cols = keep.tile([P, P], F32)
+        nc.vector.tensor_copy(out=bias_cols[:], in_=bias_bank[:, 0, :])
 
         x_rows = keep.tile([P, STREAMS * FEAT], BF16)
         h_rows = keep.tile([P, STREAMS * FEAT], BF16)
@@ -50,14 +67,12 @@ def tile_flatlstm_pa_e_kernel(
         nc.sync.dma_start(out=x_rows[:], in_=modulation)
         nc.sync.dma_start(out=h_rows[:], in_=h0)
 
-        w_planes = keep.tile([P, GROUPS, FEAT], U8, align_bytes=64)
-        nc.vector.memset(w_planes[:].bitcast(I32), 0)
         for j, (gate, words, scales, bias, func) in enumerate(gates):
             for quad in range(QUADS):
-                first = 32 * quad + 4 * j
-                nc.gpsimd.dma_start(
-                    out=w_planes[first : first + 4].bitcast(F32),
-                    in_=scales[:, 4 * quad : 4 * quad + 4, :].rearrange("g r n -> r g n").bitcast(F32),
+                top = 32 * quad + 4 * j
+                nc.sync.dma_start(
+                    out=w_planes[top : top + 4].bitcast(I32),
+                    in_=scales[:, 4 * quad : 4 * quad + 4, :].rearrange("g r n -> r g n").bitcast(I32),
                 )
 
         w_words = {}
@@ -72,74 +87,64 @@ def tile_flatlstm_pa_e_kernel(
             if s == 0:
                 nc.sync.dma_start(out=c_rows[:], in_=c0)
 
-        bias_rows = keep.tile([P, P], BF16)
-        nc.vector.memset(bias_rows[:], 0.0)
-        for j, (gate, words, scales, bias, func) in enumerate(gates):
-            nc.scalar.dma_start(
-                out=bias_rows[32 * j : 32 * (j + 1), :], in_=bias.rearrange("s (c l) -> (s c) l", l=P)
-            )
-        bias_rows_f32 = keep.tile([P, P], F32)
-        nc.vector.tensor_copy(out=bias_rows_f32[:], in_=bias_rows[:])
-        bias_bank = psum.tile([P, CHUNKS, P], F32, tag="bank")
-        nc.tensor.transpose(bias_bank[:, 0, :], bias_rows_f32[:], identity[:])
-        bias_cols = keep.tile([P, P], F32)
-        nc.vector.tensor_copy(out=bias_cols[:], in_=bias_bank[:, 0, :])
-
-        x_codes = keep.tile([P, STREAMS, HALVES * P], U32, align_bytes=64)
-        x_planes = keep.tile([P, STREAMS, HALVES * P], U8, align_bytes=64)
+        xh_codes = keep.tile([P, HALVES, STREAMS, P], U32, align_bytes=64)
+        xh_planes = keep.tile([P, HALVES, STREAMS, P], U8, align_bytes=64)
         words_in_group = FEAT // PAIR
-        for s in range(STREAMS):
-            flipped = psum.tile([P, HALVES * PAIR, P], F32, tag="bank")
-            for half, rows in enumerate((x_rows, h_rows)):
-                group_words = rows[:].bitcast(F32)[:, words_in_group * s : words_in_group * (s + 1)]
-                for u in range(PAIR):
-                    nc.tensor.transpose(flipped[:, PAIR * half + u, :], group_words[:, u::PAIR], identity[:])
-            grouped = work.tile([P, HALVES * P * PACK], BF16, align_bytes=64)
-            nc.scalar.copy(
-                out=grouped[:].bitcast(F32).rearrange("p (h n u) -> p h n u", h=HALVES, u=PAIR),
-                in_=flipped[:].rearrange("p (h u) n -> p h n u", u=PAIR),
-            )
-            nc.vector.quantize_mx(
-                out=x_codes[:, s, :].bitcast(FP8X4), scales=x_planes[:, s, :], in_=grouped[:]
-            )
-
-        for s in range(STREAMS):
-            acted = {}
-            for j, (gate, words, scales, bias, func) in enumerate(gates):
-                acc = psum.tile([P, CHUNKS, P], F32, tag="bank")
-                for c in range(CHUNKS):
-                    for half in range(HALVES):
-                        nc.tensor.matmul_mx(
-                            out=acc[:, c, :],
-                            lhsT=w_words[(gate, s)][:, half, P * c : P * (c + 1)].bitcast(FP8X4),
-                            lhsT_scale=w_planes[4 * j : P, HALVES * s + half, P * c : P * (c + 1)],
-                            rhs=x_codes[:, s, P * half : P * (half + 1)].bitcast(FP8X4),
-                            rhs_scale=x_planes[:, s, P * half : P * (half + 1)],
-                            start=(half == 0),
-                            stop=(half == HALVES - 1),
+        for half, source in enumerate((x_rows, h_rows)):
+            for first in range(0, STREAMS, 2):
+                flipped = psum.tile([P, 2 * PAIR, P], F32, tag="bank")
+                for s in (first, first + 1):
+                    group_words = source[:].bitcast(F32)[:, words_in_group * s : words_in_group * (s + 1)]
+                    for u in range(PAIR):
+                        nc.tensor.transpose(
+                            flipped[:, PAIR * (s - first) + u, :], group_words[:, u::PAIR], identity[:]
                         )
-                gate_t = work.tile([P, CHUNKS, P], F32, name="gate_%s" % gate)
-                for c in range(CHUNKS):
-                    column = 32 * j + CHUNKS * s + c
-                    nc.scalar.activation(
-                        out=gate_t[:, c, :],
-                        in_=acc[:, c, :],
-                        func=func,
-                        bias=bias_cols[:, column : column + 1],
-                        scale=1.0,
+                grouped = work.tile([P, 2 * P * PACK], BF16, align_bytes=64)
+                nc.scalar.copy(
+                    out=grouped[:].bitcast(F32).rearrange("p (s n u) -> p s n u", s=2, u=PAIR),
+                    in_=flipped[:].rearrange("p (s u) n -> p s n u", u=PAIR),
+                )
+                nc.vector.quantize_mx(
+                    out=xh_codes[:, half, first : first + 2, :].rearrange("p s n -> p (s n)").bitcast(FP8X4),
+                    scales=xh_planes[:, half, first : first + 2, :].rearrange("p s n -> p (s n)"),
+                    in_=grouped[:],
+                )
+
+        def gate_of_stream(s, j):
+            gate, words, scales, bias, func = gates[j]
+            acc = psum.tile([P, CHUNKS, P], F32, tag="bank")
+            for c in range(CHUNKS):
+                for half in range(HALVES):
+                    nc.tensor.matmul_mx(
+                        out=acc[:, c, :],
+                        lhsT=w_words[(gate, s)][:, half, P * c : P * (c + 1)].bitcast(FP8X4),
+                        lhsT_scale=w_planes[4 * j : P, HALVES * s + half, P * c : P * (c + 1)],
+                        rhs=xh_codes[:, half, s, :].bitcast(FP8X4),
+                        rhs_scale=xh_planes[:, half, s, :],
+                        start=(half == 0),
+                        stop=(half == HALVES - 1),
                     )
-                acted[gate] = gate_t
-
-            ig_t = work.tile([P, CHUNKS, P], F32)
-            nc.vector.tensor_mul(out=ig_t[:], in0=acted["i"][:], in1=acted["g"][:])
-
-            ig_rows = psum.tile([P, CHUNKS, P], F32, tag="bank")
-            f_rows = psum.tile([P, CHUNKS, P], F32, tag="bank")
+            gate_t = work.tile([P, CHUNKS, P], F32, name="gate_%s" % gate)
             for c in range(CHUNKS):
-                nc.tensor.transpose(ig_rows[:, c, :], ig_t[:, c, :], identity[:])
-            for c in range(CHUNKS):
-                nc.tensor.transpose(f_rows[:, c, :], acted["f"][:, c, :], identity[:])
+                column = 32 * j + CHUNKS * s + c
+                nc.scalar.activation(
+                    out=gate_t[:, c, :],
+                    in_=acc[:, c, :],
+                    func=func,
+                    bias=bias_cols[:, column : column + 1],
+                    scale=1.0,
+                )
+            return gate_t
 
+        def to_rows(feature_major):
+            rows = psum.tile([P, CHUNKS, P], F32, tag="bank")
+            for c in range(CHUNKS):
+                nc.tensor.transpose(rows[:, c, :], feature_major[:, c, :], identity[:])
+            return rows
+
+        def finish_stream(s, ig_t, f_t):
+            ig_rows = to_rows(ig_t)
+            f_rows = to_rows(f_t)
             stream_cols = slice(FEAT * s, FEAT * (s + 1))
             fc = work.tile([P, FEAT], F32)
             nc.vector.tensor_mul(
@@ -148,3 +153,15 @@ def tile_flatlstm_pa_e_kernel(
             c_new = done.tile([P, FEAT], F32)
             nc.vector.tensor_add(out=c_new[:], in0=fc[:], in1=ig_rows[:].rearrange("n c l -> n (c l)"))
             nc.sync.dma_start(out=out[:, stream_cols], in_=c_new[:])
+
+        unfinished = None
+        for s in range(STREAMS):
+            i_t = gate_of_stream(s, 0)
+            g_t = gate_of_stream(s, 1)
+            if unfinished is not None:
+                finish_stream(s - 1, unfinished[0], unfinished[1])
+            ig_t = work.tile([P, CHUNKS, P], F32)
+            nc.vector.tensor_mul(out=ig_t[:], in0=i_t[:], in1=g_t[:])
+            f_t = gate_of_stream(s, 2)
+            unfinished = (ig_t, f_t)
+        finish_stream(STREAMS - 1, unfinished[0], unfinished[1])

@@ -67,12 +67,11 @@ def tile_flatlstm_pa_e_kernel(
         nc.sync.dma_start(out=x_rows[:], in_=modulation)
         nc.sync.dma_start(out=h_rows[:], in_=h0)
 
-        for j, (gate, words, scales, bias, func) in enumerate(gates):
-            for quad in range(QUADS):
-                top = 32 * quad + 4 * j
+        for r in range(4):
+            for j, (gate, words, scales, bias, func) in enumerate(gates):
                 nc.sync.dma_start(
-                    out=w_planes[top : top + 4].bitcast(I32),
-                    in_=scales[:, 4 * quad : 4 * quad + 4, :].rearrange("g r n -> r g n").bitcast(I32),
+                    out=w_planes[4 * j + r : P : 32].bitcast(I32),
+                    in_=scales.rearrange("g (q r) n -> r q g n", r=4)[r].bitcast(I32),
                 )
 
         w_words = {}

@@ -47,11 +47,11 @@ def tile_flatlstm_pa_e_kernel(
 
         bias_rows = keep.tile([P, P], BF16)
         w_planes = keep.tile([P, GROUPS, FEAT], U8, align_bytes=64)
-        nc.vector.memset(bias_rows[:], 0.0)
+        nc.vector.memset(bias_rows[32 * len(gates) : P, :], 0.0)
         nc.vector.memset(w_planes[:].bitcast(I32), 0)
 
         for j, (gate, words, scales, bias, func) in enumerate(gates):
-            nc.sync.dma_start(
+            nc.scalar.dma_start(
                 out=bias_rows[32 * j : 32 * (j + 1), :], in_=bias.rearrange("s (c l) -> (s c) l", l=P)
             )
         bias_rows_f32 = keep.tile([P, P], F32)

@@ -21,6 +21,7 @@ GROUPS = STREAMS * HALVES
 CHUNKS = FEAT // P
 QUADS = 4
 PAIR = 2
+TOGETHER = 6
 
 FLOPS = 2 * P * STREAMS * (HALVES * FEAT) * FEAT * 3
 
@@ -38,7 +39,7 @@ def tile_flatlstm_pa_e_kernel(
     with ExitStack() as pools:
         keep = pools.enter_context(tc.tile_pool(name="keep", bufs=1))
         work = pools.enter_context(tc.tile_pool(name="work", bufs=3))
-        done = pools.enter_context(tc.tile_pool(name="done", bufs=STREAMS))
+        done = pools.enter_context(tc.tile_pool(name="done", bufs=STREAMS - TOGETHER))
         psum = pools.enter_context(tc.psum_pool(name="psum", bufs=8))
         pools.enter_context(tc.manual_schedule())
 
@@ -141,6 +142,8 @@ def tile_flatlstm_pa_e_kernel(
                 nc.tensor.transpose(rows[:, c, :], feature_major[:, c, :], identity[:])
             return rows
 
+        first_results = keep.tile([P, TOGETHER * FEAT], F32)
+
         def finish_stream(s, ig_t, f_t):
             ig_rows = to_rows(ig_t)
             f_rows = to_rows(f_t)
@@ -149,9 +152,16 @@ def tile_flatlstm_pa_e_kernel(
             nc.vector.tensor_mul(
                 out=fc[:], in0=f_rows[:].rearrange("n c l -> n (c l)"), in1=c_rows[:, stream_cols]
             )
-            c_new = done.tile([P, FEAT], F32)
-            nc.vector.tensor_add(out=c_new[:], in0=fc[:], in1=ig_rows[:].rearrange("n c l -> n (c l)"))
-            nc.sync.dma_start(out=out[:, stream_cols], in_=c_new[:])
+            if s < TOGETHER:
+                c_new = first_results[:, stream_cols]
+            else:
+                last_result = done.tile([P, FEAT], F32)
+                c_new = last_result[:]
+            nc.vector.tensor_add(out=c_new, in0=fc[:], in1=ig_rows[:].rearrange("n c l -> n (c l)"))
+            if s == TOGETHER - 1:
+                nc.sync.dma_start(out=out[:, 0 : TOGETHER * FEAT], in_=first_results[:])
+            elif s >= TOGETHER:
+                nc.sync.dma_start(out=out[:, stream_cols], in_=c_new)
 
         unfinished = None
         for s in range(STREAMS):

@@ -21,6 +21,7 @@ GROUPS = STREAMS * HALVES
 CHUNKS = FEAT // P
 QUADS = 4
 PAIR = 2
+LAST_PIECES = 2
 TOGETHER = 6
 
 FLOPS = 2 * P * STREAMS * (HALVES * FEAT) * FEAT * 3
@@ -136,41 +137,45 @@ def tile_flatlstm_pa_e_kernel(
                 )
             return gate_t
 
-        def to_rows(feature_major):
-            rows = psum.tile([P, CHUNKS, P], F32, tag="bank")
-            for c in range(CHUNKS):
-                nc.tensor.transpose(rows[:, c, :], feature_major[:, c, :], identity[:])
-            return rows
+        def to_rows(feature_major, chunks):
+            rows = psum.tile([P, len(chunks), P], F32, tag="bank")
+            for place, c in enumerate(chunks):
+                nc.tensor.transpose(rows[:, place, :], feature_major[:, c, :], identity[:])
+            return rows[:].rearrange("n c l -> n (c l)")
 
         first_results = keep.tile([P, TOGETHER * FEAT], F32)
 
-        def finish_stream(s, ig_t, f_t):
-            ig_rows = to_rows(ig_t)
-            f_rows = to_rows(f_t)
-            stream_cols = slice(FEAT * s, FEAT * (s + 1))
-            fc = work.tile([P, FEAT], F32)
-            nc.vector.tensor_mul(
-                out=fc[:], in0=f_rows[:].rearrange("n c l -> n (c l)"), in1=c_rows[:, stream_cols]
-            )
-            if s < TOGETHER:
-                c_new = first_results[:, stream_cols]
-            else:
-                last_result = done.tile([P, FEAT], F32)
-                c_new = last_result[:]
-            nc.vector.tensor_add(out=c_new, in0=fc[:], in1=ig_rows[:].rearrange("n c l -> n (c l)"))
+        def finish_stream(s, ig_t, f_t, pieces):
+            width = FEAT // pieces
+            chunks_of = [range(CHUNKS // pieces * n, CHUNKS // pieces * (n + 1)) for n in range(pieces)]
+            cols_of = [slice(FEAT * s + width * n, FEAT * s + width * (n + 1)) for n in range(pieces)]
+            ig_rows = to_rows(ig_t, range(CHUNKS))
+            fc_of = []
+            for n in range(pieces):
+                f_rows = to_rows(f_t, chunks_of[n])
+                fc = work.tile([P, width], F32, name="fc%d" % width)
+                nc.vector.tensor_mul(out=fc[:], in0=f_rows, in1=c_rows[:, cols_of[n]])
+                fc_of.append(fc)
+            for n in range(pieces):
+                if s < TOGETHER:
+                    c_new = first_results[:, cols_of[n]]
+                else:
+                    last_result = done.tile([P, width], F32, name="result%d" % width)
+                    c_new = last_result[:]
+                nc.vector.tensor_add(out=c_new, in0=fc_of[n][:], in1=ig_rows[:, width * n : width * (n + 1)])
+                if s >= TOGETHER:
+                    nc.sync.dma_start(out=out[:, cols_of[n]], in_=c_new)
             if s == TOGETHER - 1:
                 nc.sync.dma_start(out=out[:, 0 : TOGETHER * FEAT], in_=first_results[:])
-            elif s >= TOGETHER:
-                nc.sync.dma_start(out=out[:, stream_cols], in_=c_new)
 
         unfinished = None
         for s in range(STREAMS):
             i_t = gate_of_stream(s, 0)
-            g_t = gate_of_stream(s, 1)
             if unfinished is not None:
-                finish_stream(s - 1, unfinished[0], unfinished[1])
+                finish_stream(s - 1, unfinished[0], unfinished[1], 1)
+            g_t = gate_of_stream(s, 1)
             ig_t = work.tile([P, CHUNKS, P], F32)
             nc.vector.tensor_mul(out=ig_t[:], in0=i_t[:], in1=g_t[:])
             f_t = gate_of_stream(s, 2)
             unfinished = (ig_t, f_t)
-        finish_stream(STREAMS - 1, unfinished[0], unfinished[1])
+        finish_stream(STREAMS - 1, unfinished[0], unfinished[1], LAST_PIECES)

@@ -32,9 +32,9 @@ def tile_flatlstm_pa_e_kernel(
 ):
     nc = tc.nc
     gates = (
+        ("f", Wf_words, Wf_scales, b_f, SIGMOID),
         ("i", Wi_words, Wi_scales, b_i, SIGMOID),
         ("g", Wg_words, Wg_scales, b_g, TANH),
-        ("f", Wf_words, Wf_scales, b_f, SIGMOID),
     )
 
     with ExitStack() as pools:
@@ -111,30 +111,32 @@ def tile_flatlstm_pa_e_kernel(
                     in_=grouped[:],
                 )
 
-        def gate_of_stream(s, j):
+        def gate_of_stream(s, j, pieces=1):
             gate, words, scales, bias, func = gates[j]
-            acc = psum.tile([P, CHUNKS, P], F32, tag="bank")
-            for c in range(CHUNKS):
-                for half in range(HALVES):
-                    nc.tensor.matmul_mx(
-                        out=acc[:, c, :],
-                        lhsT=w_words[(gate, s)][:, half, P * c : P * (c + 1)].bitcast(FP8X4),
-                        lhsT_scale=w_planes[4 * j : P, HALVES * s + half, P * c : P * (c + 1)],
-                        rhs=xh_codes[:, half, s, :].bitcast(FP8X4),
-                        rhs_scale=xh_planes[:, half, s, :],
-                        start=(half == 0),
-                        stop=(half == HALVES - 1),
-                    )
             gate_t = work.tile([P, CHUNKS, P], F32, name="gate_%s" % gate)
-            for c in range(CHUNKS):
-                column = 32 * j + CHUNKS * s + c
-                nc.scalar.activation(
-                    out=gate_t[:, c, :],
-                    in_=acc[:, c, :],
-                    func=func,
-                    bias=bias_cols[:, column : column + 1],
-                    scale=1.0,
-                )
+            in_piece = CHUNKS // pieces
+            for first in range(0, CHUNKS, in_piece):
+                acc = psum.tile([P, in_piece, P], F32, tag="bank")
+                for c in range(first, first + in_piece):
+                    for half in range(HALVES):
+                        nc.tensor.matmul_mx(
+                            out=acc[:, c - first, :],
+                            lhsT=w_words[(gate, s)][:, half, P * c : P * (c + 1)].bitcast(FP8X4),
+                            lhsT_scale=w_planes[4 * j : P, HALVES * s + half, P * c : P * (c + 1)],
+                            rhs=xh_codes[:, half, s, :].bitcast(FP8X4),
+                            rhs_scale=xh_planes[:, half, s, :],
+                            start=(half == 0),
+                            stop=(half == HALVES - 1),
+                        )
+                for c in range(first, first + in_piece):
+                    column = 32 * j + CHUNKS * s + c
+                    nc.scalar.activation(
+                        out=gate_t[:, c, :],
+                        in_=acc[:, c - first, :],
+                        func=func,
+                        bias=bias_cols[:, column : column + 1],
+                        scale=1.0,
+                    )
             return gate_t
 
         def to_rows(feature_major, chunks):
@@ -145,37 +147,46 @@ def tile_flatlstm_pa_e_kernel(
 
         first_results = keep.tile([P, TOGETHER * FEAT], F32)
 
-        def finish_stream(s, ig_t, f_t, pieces):
-            width = FEAT // pieces
-            chunks_of = [range(CHUNKS // pieces * n, CHUNKS // pieces * (n + 1)) for n in range(pieces)]
-            cols_of = [slice(FEAT * s + width * n, FEAT * s + width * (n + 1)) for n in range(pieces)]
-            ig_rows = to_rows(ig_t, range(CHUNKS))
-            fc_of = []
-            for n in range(pieces):
-                f_rows = to_rows(f_t, chunks_of[n])
-                fc = work.tile([P, width], F32, name="fc%d" % width)
-                nc.vector.tensor_mul(out=fc[:], in0=f_rows, in1=c_rows[:, cols_of[n]])
-                fc_of.append(fc)
-            for n in range(pieces):
-                if s < TOGETHER:
-                    c_new = first_results[:, cols_of[n]]
-                else:
-                    last_result = done.tile([P, width], F32, name="result%d" % width)
-                    c_new = last_result[:]
-                nc.vector.tensor_add(out=c_new, in0=fc_of[n][:], in1=ig_rows[:, width * n : width * (n + 1)])
-                if s >= TOGETHER:
-                    nc.sync.dma_start(out=out[:, cols_of[n]], in_=c_new)
+        def times_c(s, f_t):
+            fc = work.tile([P, FEAT], F32)
+            nc.vector.tensor_mul(
+                out=fc[:], in0=to_rows(f_t, range(CHUNKS)), in1=c_rows[:, FEAT * s : FEAT * (s + 1)]
+            )
+            return fc
+
+        def add_and_store(s, ig_t, fc, chunks):
+            part = slice(P * chunks.start, P * chunks.stop)
+            cols = slice(FEAT * s + part.start, FEAT * s + part.stop)
+            if s < TOGETHER:
+                c_new = first_results[:, cols]
+            else:
+                last_result = done.tile([P, P * len(chunks)], F32, name="result%d" % len(chunks))
+                c_new = last_result[:]
+            nc.vector.tensor_add(out=c_new, in0=to_rows(ig_t, range(len(chunks))), in1=fc[:, part])
             if s == TOGETHER - 1:
                 nc.sync.dma_start(out=out[:, 0 : TOGETHER * FEAT], in_=first_results[:])
+            elif s >= TOGETHER:
+                nc.sync.dma_start(out=out[:, cols], in_=c_new)
 
+        size = CHUNKS // LAST_PIECES
+        pieces = [range(size * n, size * (n + 1)) for n in range(LAST_PIECES)]
         unfinished = None
         for s in range(STREAMS):
-            i_t = gate_of_stream(s, 0)
+            f_t = gate_of_stream(s, 0)
+            i_t = gate_of_stream(s, 1)
             if unfinished is not None:
-                finish_stream(s - 1, unfinished[0], unfinished[1], 1)
-            g_t = gate_of_stream(s, 1)
-            ig_t = work.tile([P, CHUNKS, P], F32)
-            nc.vector.tensor_mul(out=ig_t[:], in0=i_t[:], in1=g_t[:])
-            f_t = gate_of_stream(s, 2)
-            unfinished = (ig_t, f_t)
-        finish_stream(STREAMS - 1, unfinished[0], unfinished[1], LAST_PIECES)
+                add_and_store(s - 1, unfinished[0], unfinished[1], range(CHUNKS))
+            fc = times_c(s, f_t)
+            g_t = gate_of_stream(s, 2, LAST_PIECES if s == STREAMS - 1 else 1)
+            if s < STREAMS - 1:
+                ig_t = work.tile([P, CHUNKS, P], F32)
+                nc.vector.tensor_mul(out=ig_t[:], in0=i_t[:], in1=g_t[:])
+                unfinished = (ig_t, fc)
+        ig_of = []
+        for chunks in pieces:
+            part = slice(chunks.start, chunks.stop)
+            ig_t = work.tile([P, len(chunks), P], F32, name="ig_piece")
+            nc.vector.tensor_mul(out=ig_t[:], in0=i_t[:, part], in1=g_t[:, part])
+            ig_of.append(ig_t)
+        for chunks, ig_t in zip(pieces, ig_of):
+            add_and_store(STREAMS - 1, ig_t, fc, chunks)

from contextlib import ExitStack

import concourse.mybir as mybir
from concourse.masks import make_identity

BF16 = mybir.dt.bfloat16
F32 = mybir.dt.float32
I32 = mybir.dt.int32
U32 = mybir.dt.uint32
U8 = mybir.dt.uint8
FP8X4 = mybir.dt.float8_e4m3fn_x4
SIGMOID = mybir.ActivationFunctionType.Sigmoid
TANH = mybir.ActivationFunctionType.Tanh

P = 128
PACK = 4
STREAMS = 8
FEAT = 512
HALVES = 2
GROUPS = STREAMS * HALVES
CHUNKS = FEAT // P
QUADS = 4
PAIR = 2
LAST_PIECES = 2
TOGETHER = 6

FLOPS = 2 * P * STREAMS * (HALVES * FEAT) * FEAT * 3


def tile_flatlstm_pa_e_kernel(
    tc, modulation, h0, c0, Wi_words, Wi_scales, b_i, Wf_words, Wf_scales, b_f, Wg_words, Wg_scales, b_g, out
):
    nc = tc.nc
    gates = (
        ("f", Wf_words, Wf_scales, b_f, SIGMOID),
        ("i", Wi_words, Wi_scales, b_i, SIGMOID),
        ("g", Wg_words, Wg_scales, b_g, TANH),
    )

    with ExitStack() as pools:
        keep = pools.enter_context(tc.tile_pool(name="keep", bufs=1))
        work = pools.enter_context(tc.tile_pool(name="work", bufs=3))
        done = pools.enter_context(tc.tile_pool(name="done", bufs=STREAMS - TOGETHER))
        psum = pools.enter_context(tc.psum_pool(name="psum", bufs=8))
        pools.enter_context(tc.manual_schedule())

        identity = keep.tile([P, P], F32)
        make_identity(nc, identity[:])

        bias_rows = keep.tile([P, P], BF16)
        w_planes = keep.tile([P, GROUPS, FEAT], U8, align_bytes=64)
        nc.vector.memset(bias_rows[32 * len(gates) : P, :], 0.0)
        nc.vector.memset(w_planes[:].bitcast(I32), 0)

        for j, (gate, words, scales, bias, func) in enumerate(gates):
            nc.scalar.dma_start(
                out=bias_rows[32 * j : 32 * (j + 1), :], in_=bias.rearrange("s (c l) -> (s c) l", l=P)
            )
        bias_rows_f32 = keep.tile([P, P], F32)
        nc.vector.tensor_copy(out=bias_rows_f32[:], in_=bias_rows[:])
        bias_bank = psum.tile([P, CHUNKS, P], F32, tag="bank")
        nc.tensor.transpose(bias_bank[:, 0, :], bias_rows_f32[:], identity[:])
        bias_cols = keep.tile([P, P], F32)
        nc.vector.tensor_copy(out=bias_cols[:], in_=bias_bank[:, 0, :])

        x_rows = keep.tile([P, STREAMS * FEAT], BF16)
        h_rows = keep.tile([P, STREAMS * FEAT], BF16)
        c_rows = keep.tile([P, STREAMS * FEAT], BF16)
        nc.sync.dma_start(out=x_rows[:], in_=modulation)
        nc.sync.dma_start(out=h_rows[:], in_=h0)

        for r in range(4):
            for j, (gate, words, scales, bias, func) in enumerate(gates):
                nc.sync.dma_start(
                    out=w_planes[4 * j + r : P : 32].bitcast(I32),
                    in_=scales.rearrange("g (q r) n -> r q g n", r=4)[r].bitcast(I32),
                )

        w_words = {}
        for s in range(STREAMS):
            for gate, words, scales, bias, func in gates:
                w_tile = keep.tile([P, HALVES, FEAT], U32, name="w_%s%d" % (gate, s), align_bytes=64)
                nc.sync.dma_start(
                    out=w_tile[:].bitcast(I32),
                    in_=words[HALVES * s : HALVES * (s + 1)].rearrange("g p n t -> p g (n t)").bitcast(I32),
                )
                w_words[(gate, s)] = w_tile
            if s == 0:
                nc.sync.dma_start(out=c_rows[:], in_=c0)

        xh_codes = keep.tile([P, HALVES, STREAMS, P], U32, align_bytes=64)
        xh_planes = keep.tile([P, HALVES, STREAMS, P], U8, align_bytes=64)
        words_in_group = FEAT // PAIR
        for half, source in enumerate((x_rows, h_rows)):
            for first in range(0, STREAMS, 2):
                flipped = psum.tile([P, 2 * PAIR, P], F32, tag="bank")
                for s in (first, first + 1):
                    group_words = source[:].bitcast(F32)[:, words_in_group * s : words_in_group * (s + 1)]
                    for u in range(PAIR):
                        nc.tensor.transpose(
                            flipped[:, PAIR * (s - first) + u, :], group_words[:, u::PAIR], identity[:]
                        )
                grouped = work.tile([P, 2 * P * PACK], BF16, align_bytes=64)
                nc.scalar.copy(
                    out=grouped[:].bitcast(F32).rearrange("p (s n u) -> p s n u", s=2, u=PAIR),
                    in_=flipped[:].rearrange("p (s u) n -> p s n u", u=PAIR),
                )
                nc.vector.quantize_mx(
                    out=xh_codes[:, half, first : first + 2, :].rearrange("p s n -> p (s n)").bitcast(FP8X4),
                    scales=xh_planes[:, half, first : first + 2, :].rearrange("p s n -> p (s n)"),
                    in_=grouped[:],
                )

        def gate_of_stream(s, j, pieces=1):
            gate, words, scales, bias, func = gates[j]
            gate_t = work.tile([P, CHUNKS, P], F32, name="gate_%s" % gate)
            in_piece = CHUNKS // pieces
            for first in range(0, CHUNKS, in_piece):
                acc = psum.tile([P, in_piece, P], F32, tag="bank")
                for c in range(first, first + in_piece):
                    for half in range(HALVES):
                        nc.tensor.matmul_mx(
                            out=acc[:, c - first, :],
                            lhsT=w_words[(gate, s)][:, half, P * c : P * (c + 1)].bitcast(FP8X4),
                            lhsT_scale=w_planes[4 * j : P, HALVES * s + half, P * c : P * (c + 1)],
                            rhs=xh_codes[:, half, s, :].bitcast(FP8X4),
                            rhs_scale=xh_planes[:, half, s, :],
                            start=(half == 0),
                            stop=(half == HALVES - 1),
                        )
                for c in range(first, first + in_piece):
                    column = 32 * j + CHUNKS * s + c
                    nc.scalar.activation(
                        out=gate_t[:, c, :],
                        in_=acc[:, c - first, :],
                        func=func,
                        bias=bias_cols[:, column : column + 1],
                        scale=1.0,
                    )
            return gate_t

        def to_rows(feature_major, chunks):
            rows = psum.tile([P, len(chunks), P], F32, tag="bank")
            for place, c in enumerate(chunks):
                nc.tensor.transpose(rows[:, place, :], feature_major[:, c, :], identity[:])
            return rows[:].rearrange("n c l -> n (c l)")

        first_results = keep.tile([P, TOGETHER * FEAT], F32)

        def times_c(s, f_t):
            fc = work.tile([P, FEAT], F32)
            nc.vector.tensor_mul(
                out=fc[:], in0=to_rows(f_t, range(CHUNKS)), in1=c_rows[:, FEAT * s : FEAT * (s + 1)]
            )
            return fc

        def add_and_store(s, ig_t, fc, chunks):
            part = slice(P * chunks.start, P * chunks.stop)
            cols = slice(FEAT * s + part.start, FEAT * s + part.stop)
            if s < TOGETHER:
                c_new = first_results[:, cols]
            else:
                last_result = done.tile([P, P * len(chunks)], F32, name="result%d" % len(chunks))
                c_new = last_result[:]
            nc.vector.tensor_add(out=c_new, in0=to_rows(ig_t, range(len(chunks))), in1=fc[:, part])
            if s == TOGETHER - 1:
                nc.sync.dma_start(out=out[:, 0 : TOGETHER * FEAT], in_=first_results[:])
            elif s >= TOGETHER:
                nc.sync.dma_start(out=out[:, cols], in_=c_new)

        size = CHUNKS // LAST_PIECES
        pieces = [range(size * n, size * (n + 1)) for n in range(LAST_PIECES)]
        unfinished = None
        for s in range(STREAMS):
            f_t = gate_of_stream(s, 0)
            i_t = gate_of_stream(s, 1)
            if unfinished is not None:
                add_and_store(s - 1, unfinished[0], unfinished[1], range(CHUNKS))
            fc = times_c(s, f_t)
            g_t = gate_of_stream(s, 2, LAST_PIECES if s == STREAMS - 1 else 1)
            if s < STREAMS - 1:
                ig_t = work.tile([P, CHUNKS, P], F32)
                nc.vector.tensor_mul(out=ig_t[:], in0=i_t[:], in1=g_t[:])
                unfinished = (ig_t, fc)
        ig_of = []
        for chunks in pieces:
            part = slice(chunks.start, chunks.stop)
            ig_t = work.tile([P, len(chunks), P], F32, name="ig_piece")
            nc.vector.tensor_mul(out=ig_t[:], in0=i_t[:, part], in1=g_t[:, part])
            ig_of.append(ig_t)
        for chunks, ig_t in zip(pieces, ig_of):
            add_and_store(STREAMS - 1, ig_t, fc, chunks)
